import numpy as np
import ml_dtypes


def mxq(x, axis, fmt="e4m3"):
    dtype, down = {"e4m3": (ml_dtypes.float8_e4m3fn, 7), "e5m2": (ml_dtypes.float8_e5m2, 14)}[fmt]
    v = np.moveaxis(np.asarray(x, np.float32).astype(ml_dtypes.bfloat16).astype(np.float64), axis, -1)
    blocks = v.reshape(v.shape[:-1] + (-1, 32))
    amax = np.abs(blocks).max(-1, keepdims=True)
    byte = np.maximum(np.where(amax > 0, np.frexp(amax)[1] - 1 + 127, 0) - down, 1)
    scale = np.exp2(byte - 127.0)
    codes = (blocks / scale).astype(np.float32).astype(dtype).astype(np.float64)
    return np.moveaxis((codes * scale).reshape(v.shape), -1, axis)


WIDE = False


def mx_kscale(k):
    if not WIDE:
        return np.ones(k)
    levels = np.array([10, -10, 5, -5, 0])
    a = np.random.permutation(np.resize(levels, k // 512 * 4)).reshape(k // 512, 4)
    idx = np.arange(k)
    return np.exp2(a[idx // 512, idx % 128 // 32])


BF16 = ml_dtypes.bfloat16


def bf(x):
    return np.asarray(x, np.float32).astype(BF16)


def f64(x):
    return np.asarray(x).astype(np.float64)


N, S, K, Yd, Xd = 1024, 4, 16, 1024, 512
LOG_2PI = np.log(2.0 * np.pi)


def softplus(v):
    return np.maximum(v, 0.0) + np.log(1.0 + np.exp(-np.abs(v)))


def log_softmax(v, axis):
    m = v - v.max(axis, keepdims=True)
    return m - np.log(np.exp(m).sum(axis, keepdims=True))


def mv_gaussian_log_prob(value, mu, sig_diags, event_shape):
    diff = value - mu
    M = np.sum((diff / sig_diags) ** 2, axis=-1)
    half_log_det = np.sum(np.log(sig_diags), axis=-1)
    return -0.5 * (event_shape * LOG_2PI + M) - half_log_det


def setup_inputs():
    s = mx_kscale(Yd)
    return {"Y": bf(np.random.standard_normal((N, Yd)) * 0.5 * s),
            "We_mu": bf(np.random.standard_normal((Yd, Xd)) * 2.0 / np.sqrt(Yd) / s[:, None]),
            "be_mu": bf(np.random.standard_normal(Xd) * 0.1),
            "We_sig": bf(np.random.standard_normal((Yd, Xd)) * 1.0 / np.sqrt(Yd) / s[:, None]),
            "be_sig": bf(-3.0 + np.random.standard_normal(Xd) * 0.1),
            "phi_mus": bf(np.random.standard_normal((K, Xd)) * 3.0 / np.sqrt(Xd)),
            "phi_sigs": bf(1.0 + (np.random.random_sample((K, Xd)) - 0.5) * 9.0 / np.sqrt(Xd)),
            "phi_logits": bf(np.random.standard_normal(K))}


def reference(Y, We_mu, be_mu, We_sig, be_sig, phi_mus, phi_sigs, phi_logits):
    Yq = mxq(f64(Y), 1, "e4m3")
    enc_mu = (Yq @ mxq(f64(We_mu), 0, "e4m3")) + f64(be_mu)
    enc_sig = softplus((Yq @ mxq(f64(We_sig), 0, "e4m3")) + f64(be_sig)) + 1e-3
    log_pi = log_softmax(f64(phi_logits), -1)
    std_k = enc_sig[:, None, :] + f64(phi_sigs)[None, :, :]
    z_logits = log_pi[None, :] + mv_gaussian_log_prob(enc_mu[:, None, :], f64(phi_mus)[None, :, :], std_k, Xd)
    z_log_probs = log_softmax(z_logits, -1)
    return enc_mu, enc_sig, z_log_probs

@@ -1,0 +1,312 @@
+from contextlib import ExitStack
+
+import concourse.mybir as mybir
+from concourse.masks import make_identity
+
+F32 = mybir.dt.float32
+BF16 = mybir.dt.bfloat16
+U32 = mybir.dt.uint32
+U8 = mybir.dt.uint8
+FP8X4 = mybir.dt.float8_e4m3fn_x4
+ACT = mybir.ActivationFunctionType
+ALU = mybir.AluOpType
+AX = mybir.AxisListType
+
+P = 128
+ROWS = 1024
+KDIM = 1024
+D = 512
+CLUSTERS = 16
+ROW_TILES = ROWS // P
+D_CHUNKS = D // P
+PACK = 4
+PASSES = KDIM // (P * PACK)
+HALF = 512
+HALVES = ROWS // HALF
+BATCH = 4
+EPS = 0.001
+
+ROW_MU = 0
+ROW_SIG = CLUSTERS
+ROW_BE_MU = 2 * CLUSTERS
+ROW_BE_SIG = 2 * CLUSTERS + 1
+
+FLOPS = 2 * 2 * ROWS * KDIM * D
+
+
+def part(i, size):
+    return slice(i * size, (i + 1) * size)
+
+
+def tile_deepgmm_pa_kernel(
+    tc, Y, We_mu, be_mu, We_sig, be_sig, phi_mus, phi_sigs, phi_logits, out_0, out_1, out_2
+):
+    nc = tc.nc
+    with ExitStack() as ctx:
+        ctx.enter_context(tc.manual_schedule())
+        keep = ctx.enter_context(tc.tile_pool(name="keep", bufs=1))
+        stage = ctx.enter_context(tc.tile_pool(name="stage", bufs=4))
+        psum = ctx.enter_context(tc.psum_pool(name="psum", bufs=8))
+
+        ident_f32 = keep.tile([P, P], F32)
+        make_identity(nc, ident_f32[:])
+        ident_bf16 = keep.tile([P, P], BF16)
+        make_identity(nc, ident_bf16[:])
+        ones_col = keep.tile([P, 1], F32)
+        nc.vector.memset(ones_col[:], 1.0)
+
+        param_rows = keep.tile([P, D], BF16)
+        nc.vector.memset(param_rows[:], 0.0)
+        nc.scalar.dma_start(out=param_rows[ROW_MU : ROW_MU + CLUSTERS, :], in_=phi_mus)
+        nc.scalar.dma_start(out=param_rows[ROW_SIG : ROW_SIG + CLUSTERS, :], in_=phi_sigs)
+        nc.scalar.dma_start(out=param_rows[ROW_BE_MU : ROW_BE_MU + 1, :], in_=be_mu.unsqueeze(0))
+        nc.scalar.dma_start(out=param_rows[ROW_BE_SIG : ROW_BE_SIG + 1, :], in_=be_sig.unsqueeze(0))
+        logits_bc = keep.tile([P, CLUSTERS], BF16)
+        nc.scalar.dma_start(out=logits_bc[:], in_=phi_logits.partition_broadcast(P))
+
+        y_codes = keep.tile([P, PASSES, ROWS], U32, align_bytes=64)
+        y_scales = keep.tile([P, PASSES, ROWS], U8, align_bytes=64)
+        sig_codes = keep.tile([P, PASSES, D], U32, align_bytes=64)
+        sig_scales = keep.tile([P, PASSES, D], U8, align_bytes=64)
+        mu_codes = keep.tile([P, PASSES, D], U32, align_bytes=64)
+        mu_scales = keep.tile([P, PASSES, D], U8, align_bytes=64)
+
+        cols = keep.tile([P, D_CHUNKS, P], F32)
+        sig_t = keep.tile([P, D_CHUNKS, ROWS], F32)
+        mu_t = keep.tile([P, D_CHUNKS, ROWS], F32)
+        log_sums = keep.tile([P, CLUSTERS, ROW_TILES], F32)
+        term_sums = keep.tile([P, CLUSTERS, ROW_TILES], F32)
+
+        with tc.tile_pool(name="load", bufs=1) as load:
+            sig_raw = load.tile([P, 2 * PASSES, 2, D], BF16)
+            mu_raw = load.tile([P, 2 * PASSES, 2, D], BF16)
+            y_raw = load.tile([P, ROW_TILES, KDIM], BF16)
+            nc.sync.dma_start(
+                out=sig_raw[:], in_=We_sig.rearrange("(a q e) d -> q a e d", a=2 * PASSES, q=P, e=2)
+            )
+            y_view = Y.rearrange("(j p) y -> p j y", p=P)
+            for pair in range(ROW_TILES // 2):
+                nc.sync.dma_start(out=y_raw[:, part(pair, 2), :], in_=y_view[:, part(pair, 2), :])
+            nc.sync.dma_start(
+                out=mu_raw[:], in_=We_mu.rearrange("(a q e) d -> q a e d", a=2 * PASSES, q=P, e=2)
+            )
+
+            params_t = psum.tile([P, D_CHUNKS, P], BF16, tag="bank")
+            for c in range(D_CHUNKS):
+                nc.tensor.transpose(
+                    out=params_t[:, c, :], in_=param_rows[:, part(c, P)], identity=ident_bf16[:]
+                )
+            nc.vector.tensor_copy(out=cols[:], in_=params_t[:])
+
+            def quantise_weight(raw, grouped, codes, scales):
+                for g in range(PASSES):
+                    nc.vector.tensor_copy(
+                        out=grouped[:, g].rearrange("p d (u e) -> p d u e", u=2),
+                        in_=raw[:, part(g, 2)].rearrange("p u e d -> p d u e"),
+                    )
+                for g in range(PASSES):
+                    nc.vector.quantize_mx(
+                        out=codes[:, g, :].bitcast(FP8X4),
+                        scales=scales[:, g, :],
+                        in_=grouped[:, g].rearrange("p d t -> p (d t)"),
+                    )
+
+            sig_grouped = load.tile([P, PASSES, D, PACK], BF16, align_bytes=64)
+            quantise_weight(sig_raw, sig_grouped, sig_codes, sig_scales)
+
+            y_words = y_raw[:].bitcast(F32)
+            y_grouped = load.tile([P, PASSES, ROWS, PACK], BF16, align_bytes=64)
+            y_pairs = y_grouped[:].bitcast(F32)
+            for h in range(HALVES):
+                for pair in range(2 * h, 2 * h + 2):
+                    for g in range(PASSES):
+                        y_t = psum.tile([P, 2, 2 * P], F32, tag="bank")
+                        for u in range(2):
+                            for jj in range(2):
+                                nc.tensor.transpose(
+                                    out=y_t[:, u, part(jj, P)],
+                                    in_=y_words[:, 2 * pair + jj, part(2 * g + u, P)],
+                                    identity=ident_f32[:],
+                                )
+                        nc.scalar.copy(
+                            out=y_pairs[:, g, part(pair, 2 * P), :],
+                            in_=y_t[:].rearrange("p u n -> p n u"),
+                        )
+                for g in range(PASSES):
+                    nc.vector.quantize_mx(
+                        out=y_codes[:, g, part(h, HALF)].bitcast(FP8X4),
+                        scales=y_scales[:, g, part(h, HALF)],
+                        in_=y_grouped[:, g, part(h, HALF), :].rearrange("p n t -> p (n t)"),
+                    )
+
+            mu_grouped = load.tile([P, PASSES, D, PACK], BF16, align_bytes=64)
+            quantise_weight(mu_raw, mu_grouped, mu_codes, mu_scales)
+
+        soft = ctx.enter_context(tc.tile_pool(name="soft", bufs=1))
+        ring = ctx.enter_context(tc.tile_pool(name="ring", bufs=6))
+
+        def project(codes, scales, c, h):
+            acc = psum.tile([P, HALF], F32, tag="bank")
+            for g in range(PASSES):
+                nc.tensor.matmul_mx(
+                    out=acc[:],
+                    lhsT=codes[:, g, part(c, P)].bitcast(FP8X4),
+                    lhsT_scale=scales[:, g, part(c, P)],
+                    rhs=y_codes[:, g, part(h, HALF)].bitcast(FP8X4),
+                    rhs_scale=y_scales[:, g, part(h, HALF)],
+                    start=(g == 0),
+                    stop=(g == PASSES - 1),
+                )
+            return acc
+
+        def store_rows(src, dst):
+            for j in range(ROW_TILES):
+                rows_t = psum.tile([P, D], F32, tag="bank")
+                for c in range(D_CHUNKS):
+                    nc.tensor.transpose(
+                        out=rows_t[:, part(c, P)], in_=src[:, c, part(j, P)], identity=ident_f32[:]
+                    )
+                rows_sb = stage.tile([P, D], F32)
+                nc.vector.tensor_copy(out=rows_sb[:], in_=rows_t[:])
+                nc.sync.dma_start(out=dst[part(j, P), :], in_=rows_sb[:])
+
+        pre = soft.tile([P, D_CHUNKS, ROWS], F32)
+        ramp = soft.tile([P, D_CHUNKS, ROWS], F32)
+        tail = soft.tile([P, D_CHUNKS, ROWS], F32)
+        for h in range(HALVES):
+            for c in range(D_CHUNKS):
+                acc = project(sig_codes, sig_scales, c, h)
+                nc.vector.tensor_scalar(
+                    out=pre[:, c, part(h, HALF)],
+                    in0=acc[:],
+                    scalar1=cols[:, c, ROW_BE_SIG : ROW_BE_SIG + 1],
+                    scalar2=None,
+                    op0=ALU.add,
+                )
+        for c in range(D_CHUNKS):
+            nc.scalar.activation(out=tail[:, c, :], in_=pre[:, c, :], func=ACT.Abs)
+        nc.scalar.activation(out=tail[:], in_=tail[:], func=ACT.Exp, scale=-1.0)
+        nc.vector.tensor_scalar(
+            out=ramp[:], in0=pre[:], scalar1=0.0, scalar2=EPS, op0=ALU.max, op1=ALU.add
+        )
+        for h in range(HALVES):
+            for c in range(D_CHUNKS):
+                acc = project(mu_codes, mu_scales, c, h)
+                nc.vector.tensor_scalar(
+                    out=mu_t[:, c, part(h, HALF)],
+                    in0=acc[:],
+                    scalar1=cols[:, c, ROW_BE_MU : ROW_BE_MU + 1],
+                    scalar2=None,
+                    op0=ALU.add,
+                )
+        store_rows(mu_t, out_0)
+        for c in range(D_CHUNKS):
+            nc.scalar.activation(out=tail[:, c, :], in_=tail[:, c, :], func=ACT.Ln, bias=ones_col[:])
+            nc.vector.tensor_tensor(
+                out=sig_t[:, c, :], in0=tail[:, c, :], in1=ramp[:, c, :], op=ALU.add
+            )
+        store_rows(sig_t, out_1)
+
+        work = {}
+
+        def logs(k):
+            w = ring.tile([P, D_CHUNKS, ROWS], F32)
+            work[k] = w
+            for c in range(D_CHUNKS):
+                nc.scalar.activation(
+                    out=w[:, c, :],
+                    in_=sig_t[:, c, :],
+                    func=ACT.Ln,
+                    bias=cols[:, c, ROW_SIG + k : ROW_SIG + k + 1],
+                )
+
+        def inverse_squares(k):
+            w = work[k]
+            nc.scalar.activation(out=w[:], in_=w[:], func=ACT.Exp, scale=-2.0)
+
+        def weigh(k):
+            w = work[k]
+            for times in range(2):
+                for c in range(D_CHUNKS):
+                    nc.vector.scalar_tensor_tensor(
+                        out=w[:, c, :],
+                        in0=mu_t[:, c, :],
+                        scalar=cols[:, c, ROW_MU + k : ROW_MU + k + 1],
+                        in1=w[:, c, :],
+                        op0=ALU.subtract,
+                        op1=ALU.mult,
+                    )
+
+        def fold_chunks(k):
+            w = work[k]
+            banks = []
+            for b in range(ROW_TILES // 4):
+                folded = psum.tile([P, 4, P], F32, tag="bank")
+                banks.append(folded)
+                for jj in range(4):
+                    for c in range(D_CHUNKS):
+                        nc.tensor.matmul(
+                            out=folded[:, jj, :],
+                            lhsT=w[:, c, part(4 * b + jj, P)],
+                            rhs=ident_f32[:],
+                            is_transpose=True,
+                            start=(c == 0),
+                            stop=(c == D_CHUNKS - 1),
+                        )
+            return banks
+
+        def finish_sums(banks, sums, k):
+            for b in range(ROW_TILES // 4):
+                nc.vector.tensor_reduce(
+                    out=sums[:, k, part(b, 4)], in_=banks[b][:], axis=AX.X, op=ALU.add
+                )
+
+        log_banks = {}
+        term_banks = {}
+        for k in range(BATCH):
+            logs(k)
+            log_banks[k] = fold_chunks(k)
+        finish_sums(log_banks[0], log_sums, 0)
+        finish_sums(log_banks[1], log_sums, 1)
+        for first in range(0, CLUSTERS, BATCH):
+            for k in range(first, first + BATCH):
+                inverse_squares(k)
+            for k in range(first, first + BATCH):
+                weigh(k)
+                term_banks[k] = fold_chunks(k)
+                if k + BATCH < CLUSTERS:
+                    logs(k + BATCH)
+                    log_banks[k + BATCH] = fold_chunks(k + BATCH)
+                if k >= 1:
+                    finish_sums(term_banks[k - 1], term_sums, k - 1)
+                if k + 2 < CLUSTERS:
+                    finish_sums(log_banks[k + 2], log_sums, k + 2)
+        finish_sums(term_banks[CLUSTERS - 1], term_sums, CLUSTERS - 1)
+
+        shape = [P, ROW_TILES, CLUSTERS]
+        z = keep.tile(shape, F32)
+        nc.vector.scalar_tensor_tensor(
+            out=z[:],
+            in0=term_sums[:].rearrange("p k j -> p j k"),
+            scalar=-0.5,
+            in1=log_sums[:].rearrange("p k j -> p j k"),
+            op0=ALU.mult,
+            op1=ALU.subtract,
+        )
+        nc.vector.tensor_tensor(
+            out=z[:], in0=z[:], in1=logits_bc[:].unsqueeze(1).to_broadcast(shape), op=ALU.add
+        )
+        top = keep.tile([P, ROW_TILES], F32)
+        nc.vector.tensor_reduce(out=top[:], in_=z[:], axis=AX.X, op=ALU.max)
+        nc.vector.tensor_tensor(
+            out=z[:], in0=z[:], in1=top[:].unsqueeze(2).to_broadcast(shape), op=ALU.subtract
+        )
+        weights = keep.tile(shape, F32)
+        nc.scalar.activation(out=weights[:], in_=z[:], func=ACT.Exp)
+        norm = keep.tile([P, ROW_TILES], F32)
+        nc.vector.tensor_reduce(out=norm[:], in_=weights[:], axis=AX.X, op=ALU.add)
+        nc.scalar.activation(out=norm[:], in_=norm[:], func=ACT.Ln)
+        nc.vector.tensor_tensor(
+            out=z[:], in0=z[:], in1=norm[:].unsqueeze(2).to_broadcast(shape), op=ALU.subtract
+        )
+        nc.sync.dma_start(out=out_2.rearrange("(j p) k -> p j k", p=P), in_=z[:])

@@ -24,6 +24,7 @@ PASSES = KDIM // (P * PACK)
 HALF = 512
 HALVES = ROWS // HALF
 BATCH = 4
+TAIL_SQUARES = 3
 EPS = 0.001
 
 ROW_MU = 0
@@ -64,237 +65,291 @@ def tile_deepgmm_pa_kernel(
         logits_bc = keep.tile([P, CLUSTERS], BF16)
         nc.scalar.dma_start(out=logits_bc[:], in_=phi_logits.partition_broadcast(P))
 
-        y_codes = keep.tile([P, PASSES, ROWS], U32, align_bytes=64)
-        y_scales = keep.tile([P, PASSES, ROWS], U8, align_bytes=64)
-        sig_codes = keep.tile([P, PASSES, D], U32, align_bytes=64)
-        sig_scales = keep.tile([P, PASSES, D], U8, align_bytes=64)
-        mu_codes = keep.tile([P, PASSES, D], U32, align_bytes=64)
-        mu_scales = keep.tile([P, PASSES, D], U8, align_bytes=64)
-
         cols = keep.tile([P, D_CHUNKS, P], F32)
         sig_t = keep.tile([P, D_CHUNKS, ROWS], F32)
         mu_t = keep.tile([P, D_CHUNKS, ROWS], F32)
-        log_sums = keep.tile([P, CLUSTERS, ROW_TILES], F32)
-        term_sums = keep.tile([P, CLUSTERS, ROW_TILES], F32)
+        mu_half = keep.tile([P, D_CHUNKS, ROWS], F32)
+        half_cols = keep.tile([P, D_CHUNKS, CLUSTERS], F32)
+        neg_half_cols = keep.tile([P, D_CHUNKS, CLUSTERS], F32)
+        sums = keep.tile([P, CLUSTERS, ROW_TILES], F32)
 
-        with tc.tile_pool(name="load", bufs=1) as load:
-            sig_raw = load.tile([P, 2 * PASSES, 2, D], BF16)
-            mu_raw = load.tile([P, 2 * PASSES, 2, D], BF16)
-            y_raw = load.tile([P, ROW_TILES, KDIM], BF16)
-            nc.sync.dma_start(
-                out=sig_raw[:], in_=We_sig.rearrange("(a q e) d -> q a e d", a=2 * PASSES, q=P, e=2)
-            )
-            y_view = Y.rearrange("(j p) y -> p j y", p=P)
-            for pair in range(ROW_TILES // 2):
-                nc.sync.dma_start(out=y_raw[:, part(pair, 2), :], in_=y_view[:, part(pair, 2), :])
-            nc.sync.dma_start(
-                out=mu_raw[:], in_=We_mu.rearrange("(a q e) d -> q a e d", a=2 * PASSES, q=P, e=2)
-            )
+        with tc.tile_pool(name="codes", bufs=1) as codes_pool, tc.tile_pool(name="soft", bufs=1) as soft:
+            y_codes = codes_pool.tile([P, PASSES, ROWS], U32, align_bytes=64)
+            y_scales = codes_pool.tile([P, PASSES, ROWS], U8, align_bytes=64)
+            sig_codes = codes_pool.tile([P, PASSES, D], U32, align_bytes=64)
+            sig_scales = codes_pool.tile([P, PASSES, D], U8, align_bytes=64)
+            mu_codes = codes_pool.tile([P, PASSES, D], U32, align_bytes=64)
+            mu_scales = codes_pool.tile([P, PASSES, D], U8, align_bytes=64)
 
-            params_t = psum.tile([P, D_CHUNKS, P], BF16, tag="bank")
-            for c in range(D_CHUNKS):
-                nc.tensor.transpose(
-                    out=params_t[:, c, :], in_=param_rows[:, part(c, P)], identity=ident_bf16[:]
+            with tc.tile_pool(name="load", bufs=1) as load:
+                sig_raw = load.tile([P, 2 * PASSES, 2, D], BF16)
+                mu_raw = load.tile([P, 2 * PASSES, 2, D], BF16)
+                y_raw = load.tile([P, ROW_TILES, KDIM], BF16)
+                nc.sync.dma_start(
+                    out=sig_raw[:], in_=We_sig.rearrange("(a q e) d -> q a e d", a=2 * PASSES, q=P, e=2)
                 )
-            nc.vector.tensor_copy(out=cols[:], in_=params_t[:])
-
-            def quantise_weight(raw, grouped, codes, scales):
-                for g in range(PASSES):
-                    nc.vector.tensor_copy(
-                        out=grouped[:, g].rearrange("p d (u e) -> p d u e", u=2),
-                        in_=raw[:, part(g, 2)].rearrange("p u e d -> p d u e"),
-                    )
-                for g in range(PASSES):
-                    nc.vector.quantize_mx(
-                        out=codes[:, g, :].bitcast(FP8X4),
-                        scales=scales[:, g, :],
-                        in_=grouped[:, g].rearrange("p d t -> p (d t)"),
-                    )
-
-            sig_grouped = load.tile([P, PASSES, D, PACK], BF16, align_bytes=64)
-            quantise_weight(sig_raw, sig_grouped, sig_codes, sig_scales)
-
-            y_words = y_raw[:].bitcast(F32)
-            y_grouped = load.tile([P, PASSES, ROWS, PACK], BF16, align_bytes=64)
-            y_pairs = y_grouped[:].bitcast(F32)
-            for h in range(HALVES):
-                for pair in range(2 * h, 2 * h + 2):
-                    for g in range(PASSES):
-                        y_t = psum.tile([P, 2, 2 * P], F32, tag="bank")
-                        for u in range(2):
-                            for jj in range(2):
-                                nc.tensor.transpose(
-                                    out=y_t[:, u, part(jj, P)],
-                                    in_=y_words[:, 2 * pair + jj, part(2 * g + u, P)],
-                                    identity=ident_f32[:],
-                                )
-                        nc.scalar.copy(
-                            out=y_pairs[:, g, part(pair, 2 * P), :],
-                            in_=y_t[:].rearrange("p u n -> p n u"),
-                        )
-                for g in range(PASSES):
-                    nc.vector.quantize_mx(
-                        out=y_codes[:, g, part(h, HALF)].bitcast(FP8X4),
-                        scales=y_scales[:, g, part(h, HALF)],
-                        in_=y_grouped[:, g, part(h, HALF), :].rearrange("p n t -> p (n t)"),
-                    )
-
-            mu_grouped = load.tile([P, PASSES, D, PACK], BF16, align_bytes=64)
-            quantise_weight(mu_raw, mu_grouped, mu_codes, mu_scales)
-
-        soft = ctx.enter_context(tc.tile_pool(name="soft", bufs=1))
-        ring = ctx.enter_context(tc.tile_pool(name="ring", bufs=6))
-
-        def project(codes, scales, c, h):
-            acc = psum.tile([P, HALF], F32, tag="bank")
-            for g in range(PASSES):
-                nc.tensor.matmul_mx(
-                    out=acc[:],
-                    lhsT=codes[:, g, part(c, P)].bitcast(FP8X4),
-                    lhsT_scale=scales[:, g, part(c, P)],
-                    rhs=y_codes[:, g, part(h, HALF)].bitcast(FP8X4),
-                    rhs_scale=y_scales[:, g, part(h, HALF)],
-                    start=(g == 0),
-                    stop=(g == PASSES - 1),
+                y_view = Y.rearrange("(j p) y -> p j y", p=P)
+                for pair in range(ROW_TILES // 2):
+                    nc.sync.dma_start(out=y_raw[:, part(pair, 2), :], in_=y_view[:, part(pair, 2), :])
+                nc.sync.dma_start(
+                    out=mu_raw[:], in_=We_mu.rearrange("(a q e) d -> q a e d", a=2 * PASSES, q=P, e=2)
                 )
-            return acc
 
-        def store_rows(src, dst):
-            for j in range(ROW_TILES):
-                rows_t = psum.tile([P, D], F32, tag="bank")
+                params_t = psum.tile([P, D_CHUNKS, P], BF16, tag="bank")
                 for c in range(D_CHUNKS):
                     nc.tensor.transpose(
-                        out=rows_t[:, part(c, P)], in_=src[:, c, part(j, P)], identity=ident_f32[:]
+                        out=params_t[:, c, :], in_=param_rows[:, part(c, P)], identity=ident_bf16[:]
                     )
-                rows_sb = stage.tile([P, D], F32)
-                nc.vector.tensor_copy(out=rows_sb[:], in_=rows_t[:])
-                nc.sync.dma_start(out=dst[part(j, P), :], in_=rows_sb[:])
+                nc.vector.tensor_copy(out=cols[:], in_=params_t[:])
+                nc.vector.tensor_scalar(
+                    out=half_cols[:],
+                    in0=cols[:, :, ROW_MU : ROW_MU + CLUSTERS],
+                    scalar1=0.5,
+                    scalar2=None,
+                    op0=ALU.mult,
+                )
+                nc.vector.tensor_scalar(
+                    out=neg_half_cols[:],
+                    in0=cols[:, :, ROW_MU : ROW_MU + CLUSTERS],
+                    scalar1=-0.5,
+                    scalar2=None,
+                    op0=ALU.mult,
+                )
 
-        pre = soft.tile([P, D_CHUNKS, ROWS], F32)
-        ramp = soft.tile([P, D_CHUNKS, ROWS], F32)
-        tail = soft.tile([P, D_CHUNKS, ROWS], F32)
-        for h in range(HALVES):
+                def quantise_weight(raw, grouped, codes, scales):
+                    for g in range(PASSES):
+                        nc.vector.tensor_copy(
+                            out=grouped[:, g].rearrange("p d (u e) -> p d u e", u=2),
+                            in_=raw[:, part(g, 2)].rearrange("p u e d -> p d u e"),
+                        )
+                    for g in range(PASSES):
+                        nc.vector.quantize_mx(
+                            out=codes[:, g, :].bitcast(FP8X4),
+                            scales=scales[:, g, :],
+                            in_=grouped[:, g].rearrange("p d t -> p (d t)"),
+                        )
+
+                sig_grouped = load.tile([P, PASSES, D, PACK], BF16, align_bytes=64)
+                quantise_weight(sig_raw, sig_grouped, sig_codes, sig_scales)
+
+                y_words = y_raw[:].bitcast(F32)
+                y_grouped = load.tile([P, PASSES, ROWS, PACK], BF16, align_bytes=64)
+                y_pairs = y_grouped[:].bitcast(F32)
+                for h in range(HALVES):
+                    for pair in range(2 * h, 2 * h + 2):
+                        for g in range(PASSES):
+                            y_t = psum.tile([P, 2, 2 * P], F32, tag="bank")
+                            for u in range(2):
+                                for jj in range(2):
+                                    nc.tensor.transpose(
+                                        out=y_t[:, u, part(jj, P)],
+                                        in_=y_words[:, 2 * pair + jj, part(2 * g + u, P)],
+                                        identity=ident_f32[:],
+                                    )
+                            nc.scalar.copy(
+                                out=y_pairs[:, g, part(pair, 2 * P), :],
+                                in_=y_t[:].rearrange("p u n -> p n u"),
+                            )
+                    for g in range(PASSES):
+                        nc.vector.quantize_mx(
+                            out=y_codes[:, g, part(h, HALF)].bitcast(FP8X4),
+                            scales=y_scales[:, g, part(h, HALF)],
+                            in_=y_grouped[:, g, part(h, HALF), :].rearrange("p n t -> p (n t)"),
+                        )
+
+                mu_grouped = load.tile([P, PASSES, D, PACK], BF16, align_bytes=64)
+                quantise_weight(mu_raw, mu_grouped, mu_codes, mu_scales)
+
+            def project(codes, scales, c, h):
+                acc = psum.tile([P, HALF], F32, tag="bank")
+                for g in range(PASSES):
+                    nc.tensor.matmul_mx(
+                        out=acc[:],
+                        lhsT=codes[:, g, part(c, P)].bitcast(FP8X4),
+                        lhsT_scale=scales[:, g, part(c, P)],
+                        rhs=y_codes[:, g, part(h, HALF)].bitcast(FP8X4),
+                        rhs_scale=y_scales[:, g, part(h, HALF)],
+                        start=(g == 0),
+                        stop=(g == PASSES - 1),
+                    )
+                return acc
+
+            def store_rows(src, dst):
+                for j in range(ROW_TILES):
+                    rows_t = psum.tile([P, D], F32, tag="bank")
+                    for c in range(D_CHUNKS):
+                        nc.tensor.transpose(
+                            out=rows_t[:, part(c, P)], in_=src[:, c, part(j, P)], identity=ident_f32[:]
+                        )
+                    rows_sb = stage.tile([P, D], F32)
+                    nc.vector.tensor_copy(out=rows_sb[:], in_=rows_t[:])
+                    nc.sync.dma_start(out=dst[part(j, P), :], in_=rows_sb[:])
+
+            pre = soft.tile([P, D_CHUNKS, ROWS], F32)
+            ramp = soft.tile([P, D_CHUNKS, ROWS], F32)
+            tail = soft.tile([P, D_CHUNKS, ROWS], F32)
+            for h in range(HALVES):
+                for c in range(D_CHUNKS):
+                    acc = project(sig_codes, sig_scales, c, h)
+                    nc.vector.tensor_scalar(
+                        out=pre[:, c, part(h, HALF)],
+                        in0=acc[:],
+                        scalar1=cols[:, c, ROW_BE_SIG : ROW_BE_SIG + 1],
+                        scalar2=None,
+                        op0=ALU.add,
+                    )
             for c in range(D_CHUNKS):
-                acc = project(sig_codes, sig_scales, c, h)
-                nc.vector.tensor_scalar(
-                    out=pre[:, c, part(h, HALF)],
-                    in0=acc[:],
-                    scalar1=cols[:, c, ROW_BE_SIG : ROW_BE_SIG + 1],
-                    scalar2=None,
-                    op0=ALU.add,
-                )
-        for c in range(D_CHUNKS):
-            nc.scalar.activation(out=tail[:, c, :], in_=pre[:, c, :], func=ACT.Abs)
-        nc.scalar.activation(out=tail[:], in_=tail[:], func=ACT.Exp, scale=-1.0)
-        nc.vector.tensor_scalar(
-            out=ramp[:], in0=pre[:], scalar1=0.0, scalar2=EPS, op0=ALU.max, op1=ALU.add
-        )
-        for h in range(HALVES):
-            for c in range(D_CHUNKS):
-                acc = project(mu_codes, mu_scales, c, h)
-                nc.vector.tensor_scalar(
-                    out=mu_t[:, c, part(h, HALF)],
-                    in0=acc[:],
-                    scalar1=cols[:, c, ROW_BE_MU : ROW_BE_MU + 1],
-                    scalar2=None,
-                    op0=ALU.add,
-                )
-        store_rows(mu_t, out_0)
-        for c in range(D_CHUNKS):
-            nc.scalar.activation(out=tail[:, c, :], in_=tail[:, c, :], func=ACT.Ln, bias=ones_col[:])
-            nc.vector.tensor_tensor(
-                out=sig_t[:, c, :], in0=tail[:, c, :], in1=ramp[:, c, :], op=ALU.add
+                nc.scalar.activation(out=tail[:, c, :], in_=pre[:, c, :], func=ACT.Abs)
+            nc.scalar.activation(out=tail[:], in_=tail[:], func=ACT.Exp, scale=-1.0)
+            nc.vector.tensor_scalar(
+                out=ramp[:], in0=pre[:], scalar1=0.0, scalar2=EPS, op0=ALU.max, op1=ALU.add
             )
-        store_rows(sig_t, out_1)
+            for h in range(HALVES):
+                for c in range(D_CHUNKS):
+                    acc = project(mu_codes, mu_scales, c, h)
+                    nc.vector.tensor_scalar(
+                        out=mu_t[:, c, part(h, HALF)],
+                        in0=acc[:],
+                        scalar1=cols[:, c, ROW_BE_MU : ROW_BE_MU + 1],
+                        scalar2=None,
+                        op0=ALU.add,
+                    )
+            nc.vector.tensor_scalar(
+                out=mu_half[:], in0=mu_t[:], scalar1=0.5, scalar2=None, op0=ALU.mult
+            )
+            store_rows(mu_t, out_0)
+            for c in range(D_CHUNKS):
+                nc.scalar.activation(out=tail[:, c, :], in_=tail[:, c, :], func=ACT.Ln, bias=ones_col[:])
+                nc.vector.tensor_tensor(
+                    out=sig_t[:, c, :], in0=tail[:, c, :], in1=ramp[:, c, :], op=ALU.add
+                )
+            store_rows(sig_t, out_1)
 
-        work = {}
+
+        log_ring = ctx.enter_context(tc.tile_pool(name="log_ring", bufs=6))
+        term_ring = ctx.enter_context(tc.tile_pool(name="term_ring", bufs=4))
+        log_tiles = {}
+        term_tiles = {}
+        banks = {}
+        square_tiles = {}
 
         def logs(k):
-            w = ring.tile([P, D_CHUNKS, ROWS], F32)
-            work[k] = w
+            log_std = log_ring.tile([P, D_CHUNKS, ROWS], F32)
+            log_tiles[k] = log_std
             for c in range(D_CHUNKS):
                 nc.scalar.activation(
-                    out=w[:, c, :],
+                    out=log_std[:, c, :],
                     in_=sig_t[:, c, :],
                     func=ACT.Ln,
                     bias=cols[:, c, ROW_SIG + k : ROW_SIG + k + 1],
                 )
 
         def inverse_squares(k):
-            w = work[k]
-            nc.scalar.activation(out=w[:], in_=w[:], func=ACT.Exp, scale=-2.0)
+            term = term_ring.tile([P, D_CHUNKS, ROWS], F32)
+            term_tiles[k] = term
+            for c in range(D_CHUNKS):
+                nc.scalar.activation(
+                    out=term[:, c, :], in_=log_tiles[k][:, c, :], func=ACT.Exp, scale=-2.0
+                )
+
+        def scalar_squares(k):
+            return CLUSTERS - TAIL_SQUARES <= k < CLUSTERS
+
+        def quarter_squares(k):
+            quarter = log_ring.tile([P, D_CHUNKS, ROWS], F32, tag="log_std")
+            square_tiles[k] = quarter
+            for c in range(D_CHUNKS):
+                nc.scalar.activation(
+                    out=quarter[:, c, :],
+                    in_=mu_half[:, c, :],
+                    func=ACT.Square,
+                    bias=neg_half_cols[:, c, k : k + 1],
+                )
+
+        def weigh_squares(k):
+            term = term_tiles[k]
+            nc.vector.scalar_tensor_tensor(
+                out=term[:].rearrange("p c n -> p (c n)"),
+                in0=square_tiles[k][:].rearrange("p c n -> p (c n)"),
+                scalar=2.0,
+                in1=term[:].rearrange("p c n -> p (c n)"),
+                op0=ALU.mult,
+                op1=ALU.mult,
+            )
 
         def weigh(k):
-            w = work[k]
-            for times in range(2):
-                for c in range(D_CHUNKS):
-                    nc.vector.scalar_tensor_tensor(
-                        out=w[:, c, :],
-                        in0=mu_t[:, c, :],
-                        scalar=cols[:, c, ROW_MU + k : ROW_MU + k + 1],
-                        in1=w[:, c, :],
-                        op0=ALU.subtract,
-                        op1=ALU.mult,
-                    )
+            term = term_tiles[k]
+            for c in range(D_CHUNKS):
+                nc.vector.scalar_tensor_tensor(
+                    out=term[:, c, :],
+                    in0=mu_t[:, c, :],
+                    scalar=cols[:, c, ROW_MU + k : ROW_MU + k + 1],
+                    in1=term[:, c, :],
+                    op0=ALU.subtract,
+                    op1=ALU.mult,
+                )
+            for c in range(D_CHUNKS):
+                nc.vector.scalar_tensor_tensor(
+                    out=term[:, c, :],
+                    in0=mu_half[:, c, :],
+                    scalar=half_cols[:, c, k : k + 1],
+                    in1=term[:, c, :],
+                    op0=ALU.subtract,
+                    op1=ALU.mult,
+                )
 
-        def fold_chunks(k):
-            w = work[k]
-            banks = []
+        def fold(src, k, opens, closes):
             for b in range(ROW_TILES // 4):
-                folded = psum.tile([P, 4, P], F32, tag="bank")
-                banks.append(folded)
                 for jj in range(4):
                     for c in range(D_CHUNKS):
                         nc.tensor.matmul(
-                            out=folded[:, jj, :],
-                            lhsT=w[:, c, part(4 * b + jj, P)],
+                            out=banks[k][b][:, jj, :],
+                            lhsT=src[:, c, part(4 * b + jj, P)],
                             rhs=ident_f32[:],
                             is_transpose=True,
-                            start=(c == 0),
-                            stop=(c == D_CHUNKS - 1),
+                            start=(opens and jj == 0 and c == 0),
+                            stop=(closes and jj == 3 and c == D_CHUNKS - 1),
                         )
-            return banks
 
-        def finish_sums(banks, sums, k):
+        def fold_logs(k):
+            bank_a = psum.tile([P, 4, P], F32, tag="bank")
+            bank_b = psum.tile([P, 4, P], F32, tag="bank")
+            banks[k] = [bank_a, bank_b]
+            fold(log_tiles[k], k, True, False)
+
+        def finish_sums(k):
             for b in range(ROW_TILES // 4):
                 nc.vector.tensor_reduce(
-                    out=sums[:, k, part(b, 4)], in_=banks[b][:], axis=AX.X, op=ALU.add
+                    out=sums[:, k, part(b, 4)], in_=banks[k][b][:], axis=AX.X, op=ALU.add
                 )
 
-        log_banks = {}
-        term_banks = {}
         for k in range(BATCH):
             logs(k)
-            log_banks[k] = fold_chunks(k)
-        finish_sums(log_banks[0], log_sums, 0)
-        finish_sums(log_banks[1], log_sums, 1)
         for first in range(0, CLUSTERS, BATCH):
             for k in range(first, first + BATCH):
                 inverse_squares(k)
             for k in range(first, first + BATCH):
-                weigh(k)
-                term_banks[k] = fold_chunks(k)
+                fold_logs(k)
+                if scalar_squares(k):
+                    weigh_squares(k)
+                else:
+                    weigh(k)
+                fold(term_tiles[k], k, False, True)
                 if k + BATCH < CLUSTERS:
                     logs(k + BATCH)
-                    log_banks[k + BATCH] = fold_chunks(k + BATCH)
+                elif scalar_squares(k + 1):
+                    quarter_squares(k + 1)
                 if k >= 1:
-                    finish_sums(term_banks[k - 1], term_sums, k - 1)
-                if k + 2 < CLUSTERS:
-                    finish_sums(log_banks[k + 2], log_sums, k + 2)
-        finish_sums(term_banks[CLUSTERS - 1], term_sums, CLUSTERS - 1)
+                    finish_sums(k - 1)
+        finish_sums(CLUSTERS - 1)
 
         shape = [P, ROW_TILES, CLUSTERS]
         z = keep.tile(shape, F32)
-        nc.vector.scalar_tensor_tensor(
-            out=z[:],
-            in0=term_sums[:].rearrange("p k j -> p j k"),
-            scalar=-0.5,
-            in1=log_sums[:].rearrange("p k j -> p j k"),
-            op0=ALU.mult,
-            op1=ALU.subtract,
-        )
         nc.vector.tensor_tensor(
-            out=z[:], in0=z[:], in1=logits_bc[:].unsqueeze(1).to_broadcast(shape), op=ALU.add
+            out=z[:],
+            in0=logits_bc[:].unsqueeze(1).to_broadcast(shape),
+            in1=sums[:].rearrange("p k j -> p j k"),
+            op=ALU.subtract,
         )
         top = keep.tile([P, ROW_TILES], F32)
         nc.vector.tensor_reduce(out=top[:], in_=z[:], axis=AX.X, op=ALU.max)

@@ -24,7 +24,8 @@ PASSES = KDIM // (P * PACK)
 HALF = 512
 HALVES = ROWS // HALF
 BATCH = 4
-TAIL_SQUARES = 3
+LOGS_AHEAD = 2
+TAIL_SQUARES = 2
 EPS = 0.001
 
 ROW_MU = 0
@@ -73,7 +74,10 @@ def tile_deepgmm_pa_kernel(
         neg_half_cols = keep.tile([P, D_CHUNKS, CLUSTERS], F32)
         sums = keep.tile([P, CLUSTERS, ROW_TILES], F32)
 
-        with tc.tile_pool(name="codes", bufs=1) as codes_pool, tc.tile_pool(name="soft", bufs=1) as soft:
+        with ExitStack() as head:
+            codes_pool = head.enter_context(tc.tile_pool(name="codes", bufs=1))
+            soft = head.enter_context(tc.tile_pool(name="soft", bufs=1))
+            load = head.enter_context(tc.tile_pool(name="load", bufs=1))
             y_codes = codes_pool.tile([P, PASSES, ROWS], U32, align_bytes=64)
             y_scales = codes_pool.tile([P, PASSES, ROWS], U8, align_bytes=64)
             sig_codes = codes_pool.tile([P, PASSES, D], U32, align_bytes=64)
@@ -81,84 +85,80 @@ def tile_deepgmm_pa_kernel(
             mu_codes = codes_pool.tile([P, PASSES, D], U32, align_bytes=64)
             mu_scales = codes_pool.tile([P, PASSES, D], U8, align_bytes=64)
 
-            with tc.tile_pool(name="load", bufs=1) as load:
-                sig_raw = load.tile([P, 2 * PASSES, 2, D], BF16)
-                mu_raw = load.tile([P, 2 * PASSES, 2, D], BF16)
-                y_raw = load.tile([P, ROW_TILES, KDIM], BF16)
-                nc.sync.dma_start(
-                    out=sig_raw[:], in_=We_sig.rearrange("(a q e) d -> q a e d", a=2 * PASSES, q=P, e=2)
-                )
-                y_view = Y.rearrange("(j p) y -> p j y", p=P)
-                for pair in range(ROW_TILES // 2):
-                    nc.sync.dma_start(out=y_raw[:, part(pair, 2), :], in_=y_view[:, part(pair, 2), :])
-                nc.sync.dma_start(
-                    out=mu_raw[:], in_=We_mu.rearrange("(a q e) d -> q a e d", a=2 * PASSES, q=P, e=2)
-                )
+            sig_raw = load.tile([P, 2 * PASSES, 2, D], BF16)
+            mu_raw = load.tile([P, 2 * PASSES, 2, D], BF16)
+            y_raw = load.tile([P, ROW_TILES, KDIM], BF16)
+            nc.sync.dma_start(
+                out=sig_raw[:], in_=We_sig.rearrange("(a q e) d -> q a e d", a=2 * PASSES, q=P, e=2)
+            )
+            y_view = Y.rearrange("(j p) y -> p j y", p=P)
+            for pair in range(ROW_TILES // 2):
+                nc.sync.dma_start(out=y_raw[:, part(pair, 2), :], in_=y_view[:, part(pair, 2), :])
+            nc.sync.dma_start(
+                out=mu_raw[:], in_=We_mu.rearrange("(a q e) d -> q a e d", a=2 * PASSES, q=P, e=2)
+            )
 
-                params_t = psum.tile([P, D_CHUNKS, P], BF16, tag="bank")
-                for c in range(D_CHUNKS):
-                    nc.tensor.transpose(
-                        out=params_t[:, c, :], in_=param_rows[:, part(c, P)], identity=ident_bf16[:]
+            params_t = psum.tile([P, D_CHUNKS, P], BF16, tag="bank")
+            for c in range(D_CHUNKS):
+                nc.tensor.transpose(
+                    out=params_t[:, c, :], in_=param_rows[:, part(c, P)], identity=ident_bf16[:]
+                )
+            nc.vector.tensor_copy(out=cols[:], in_=params_t[:])
+            nc.vector.tensor_scalar(
+                out=half_cols[:],
+                in0=cols[:, :, ROW_MU : ROW_MU + CLUSTERS],
+                scalar1=0.5,
+                scalar2=None,
+                op0=ALU.mult,
+            )
+            nc.vector.tensor_scalar(
+                out=neg_half_cols[:],
+                in0=cols[:, :, ROW_MU : ROW_MU + CLUSTERS],
+                scalar1=-0.5,
+                scalar2=None,
+                op0=ALU.mult,
+            )
+
+            def quantise_weight(raw, grouped, codes, scales):
+                for g in range(PASSES):
+                    nc.vector.tensor_copy(
+                        out=grouped[:, g].rearrange("p d (u e) -> p d u e", u=2),
+                        in_=raw[:, part(g, 2)].rearrange("p u e d -> p d u e"),
                     )
-                nc.vector.tensor_copy(out=cols[:], in_=params_t[:])
-                nc.vector.tensor_scalar(
-                    out=half_cols[:],
-                    in0=cols[:, :, ROW_MU : ROW_MU + CLUSTERS],
-                    scalar1=0.5,
-                    scalar2=None,
-                    op0=ALU.mult,
-                )
-                nc.vector.tensor_scalar(
-                    out=neg_half_cols[:],
-                    in0=cols[:, :, ROW_MU : ROW_MU + CLUSTERS],
-                    scalar1=-0.5,
-                    scalar2=None,
-                    op0=ALU.mult,
-                )
+                for g in range(PASSES):
+                    nc.vector.quantize_mx(
+                        out=codes[:, g, :].bitcast(FP8X4),
+                        scales=scales[:, g, :],
+                        in_=grouped[:, g].rearrange("p d t -> p (d t)"),
+                    )
 
-                def quantise_weight(raw, grouped, codes, scales):
+            sig_grouped = load.tile([P, PASSES, D, PACK], BF16, align_bytes=64)
+            quantise_weight(sig_raw, sig_grouped, sig_codes, sig_scales)
+
+            y_words = y_raw[:].bitcast(F32)
+            y_grouped = load.tile([P, PASSES, ROWS, PACK], BF16, align_bytes=64)
+            y_pairs = y_grouped[:].bitcast(F32)
+            for h in range(HALVES):
+                for pair in range(2 * h, 2 * h + 2):
                     for g in range(PASSES):
-                        nc.vector.tensor_copy(
-                            out=grouped[:, g].rearrange("p d (u e) -> p d u e", u=2),
-                            in_=raw[:, part(g, 2)].rearrange("p u e d -> p d u e"),
+                        y_t = psum.tile([P, 2, 2 * P], F32, tag="bank")
+                        for u in range(2):
+                            for jj in range(2):
+                                nc.tensor.transpose(
+                                    out=y_t[:, u, part(jj, P)],
+                                    in_=y_words[:, 2 * pair + jj, part(2 * g + u, P)],
+                                    identity=ident_f32[:],
+                                )
+                        nc.scalar.copy(
+                            out=y_pairs[:, g, part(pair, 2 * P), :],
+                            in_=y_t[:].rearrange("p u n -> p n u"),
                         )
-                    for g in range(PASSES):
-                        nc.vector.quantize_mx(
-                            out=codes[:, g, :].bitcast(FP8X4),
-                            scales=scales[:, g, :],
-                            in_=grouped[:, g].rearrange("p d t -> p (d t)"),
-                        )
-
-                sig_grouped = load.tile([P, PASSES, D, PACK], BF16, align_bytes=64)
-                quantise_weight(sig_raw, sig_grouped, sig_codes, sig_scales)
-
-                y_words = y_raw[:].bitcast(F32)
-                y_grouped = load.tile([P, PASSES, ROWS, PACK], BF16, align_bytes=64)
-                y_pairs = y_grouped[:].bitcast(F32)
-                for h in range(HALVES):
-                    for pair in range(2 * h, 2 * h + 2):
-                        for g in range(PASSES):
-                            y_t = psum.tile([P, 2, 2 * P], F32, tag="bank")
-                            for u in range(2):
-                                for jj in range(2):
-                                    nc.tensor.transpose(
-                                        out=y_t[:, u, part(jj, P)],
-                                        in_=y_words[:, 2 * pair + jj, part(2 * g + u, P)],
-                                        identity=ident_f32[:],
-                                    )
-                            nc.scalar.copy(
-                                out=y_pairs[:, g, part(pair, 2 * P), :],
-                                in_=y_t[:].rearrange("p u n -> p n u"),
-                            )
-                    for g in range(PASSES):
-                        nc.vector.quantize_mx(
-                            out=y_codes[:, g, part(h, HALF)].bitcast(FP8X4),
-                            scales=y_scales[:, g, part(h, HALF)],
-                            in_=y_grouped[:, g, part(h, HALF), :].rearrange("p n t -> p (n t)"),
-                        )
-
-                mu_grouped = load.tile([P, PASSES, D, PACK], BF16, align_bytes=64)
-                quantise_weight(mu_raw, mu_grouped, mu_codes, mu_scales)
+                for g in range(PASSES):
+                    nc.vector.quantize_mx(
+                        out=y_codes[:, g, part(h, HALF)].bitcast(FP8X4),
+                        scales=y_scales[:, g, part(h, HALF)],
+                        in_=y_grouped[:, g, part(h, HALF), :].rearrange("p n t -> p (n t)"),
+                    )
 
             def project(codes, scales, c, h):
                 acc = psum.tile([P, HALF], F32, tag="bank")
@@ -174,17 +174,6 @@ def tile_deepgmm_pa_kernel(
                     )
                 return acc
 
-            def store_rows(src, dst):
-                for j in range(ROW_TILES):
-                    rows_t = psum.tile([P, D], F32, tag="bank")
-                    for c in range(D_CHUNKS):
-                        nc.tensor.transpose(
-                            out=rows_t[:, part(c, P)], in_=src[:, c, part(j, P)], identity=ident_f32[:]
-                        )
-                    rows_sb = stage.tile([P, D], F32)
-                    nc.vector.tensor_copy(out=rows_sb[:], in_=rows_t[:])
-                    nc.sync.dma_start(out=dst[part(j, P), :], in_=rows_sb[:])
-
             pre = soft.tile([P, D_CHUNKS, ROWS], F32)
             ramp = soft.tile([P, D_CHUNKS, ROWS], F32)
             tail = soft.tile([P, D_CHUNKS, ROWS], F32)
@@ -198,12 +187,22 @@ def tile_deepgmm_pa_kernel(
                         scalar2=None,
                         op0=ALU.add,
                     )
-            for c in range(D_CHUNKS):
-                nc.scalar.activation(out=tail[:, c, :], in_=pre[:, c, :], func=ACT.Abs)
-            nc.scalar.activation(out=tail[:], in_=tail[:], func=ACT.Exp, scale=-1.0)
+                    nc.scalar.activation(
+                        out=tail[:, c, part(h, HALF)], in_=pre[:, c, part(h, HALF)], func=ACT.Abs
+                    )
+                nc.scalar.activation(
+                    out=tail[:, :, part(h, HALF)], in_=tail[:, :, part(h, HALF)], func=ACT.Exp, scale=-1.0
+                )
             nc.vector.tensor_scalar(
                 out=ramp[:], in0=pre[:], scalar1=0.0, scalar2=EPS, op0=ALU.max, op1=ALU.add
             )
+            mu_grouped = load.tile([P, PASSES, D, PACK], BF16, align_bytes=64)
+            quantise_weight(mu_raw, mu_grouped, mu_codes, mu_scales)
+            for c in range(D_CHUNKS):
+                nc.scalar.activation(out=tail[:, c, :], in_=tail[:, c, :], func=ACT.Ln, bias=ones_col[:])
+                nc.vector.tensor_tensor(
+                    out=sig_t[:, c, :], in0=tail[:, c, :], in1=ramp[:, c, :], op=ALU.add
+                )
             for h in range(HALVES):
                 for c in range(D_CHUNKS):
                     acc = project(mu_codes, mu_scales, c, h)
@@ -214,24 +213,24 @@ def tile_deepgmm_pa_kernel(
                         scalar2=None,
                         op0=ALU.add,
                     )
-            nc.vector.tensor_scalar(
-                out=mu_half[:], in0=mu_t[:], scalar1=0.5, scalar2=None, op0=ALU.mult
-            )
-            store_rows(mu_t, out_0)
-            for c in range(D_CHUNKS):
-                nc.scalar.activation(out=tail[:, c, :], in_=tail[:, c, :], func=ACT.Ln, bias=ones_col[:])
-                nc.vector.tensor_tensor(
-                    out=sig_t[:, c, :], in0=tail[:, c, :], in1=ramp[:, c, :], op=ALU.add
-                )
-            store_rows(sig_t, out_1)
 
+        def store_rows(src, dst):
+            for j in range(ROW_TILES):
+                rows_t = psum.tile([P, D], F32, tag="bank")
+                for c in range(D_CHUNKS):
+                    nc.tensor.transpose(
+                        out=rows_t[:, part(c, P)], in_=src[:, c, part(j, P)], identity=ident_f32[:]
+                    )
+                rows_sb = stage.tile([P, D], F32)
+                nc.vector.tensor_copy(out=rows_sb[:], in_=rows_t[:])
+                nc.sync.dma_start(out=dst[part(j, P), :], in_=rows_sb[:])
 
         log_ring = ctx.enter_context(tc.tile_pool(name="log_ring", bufs=6))
         term_ring = ctx.enter_context(tc.tile_pool(name="term_ring", bufs=4))
         log_tiles = {}
         term_tiles = {}
-        banks = {}
         square_tiles = {}
+        banks = {}
 
         def logs(k):
             log_std = log_ring.tile([P, D_CHUNKS, ROWS], F32)
@@ -268,14 +267,15 @@ def tile_deepgmm_pa_kernel(
 
         def weigh_squares(k):
             term = term_tiles[k]
-            nc.vector.scalar_tensor_tensor(
-                out=term[:].rearrange("p c n -> p (c n)"),
-                in0=square_tiles[k][:].rearrange("p c n -> p (c n)"),
-                scalar=2.0,
-                in1=term[:].rearrange("p c n -> p (c n)"),
-                op0=ALU.mult,
-                op1=ALU.mult,
-            )
+            for c in range(D_CHUNKS):
+                nc.vector.scalar_tensor_tensor(
+                    out=term[:, c, :],
+                    in0=square_tiles[k][:, c, :],
+                    scalar=2.0,
+                    in1=term[:, c, :],
+                    op0=ALU.mult,
+                    op1=ALU.mult,
+                )
 
         def weigh(k):
             term = term_tiles[k]
@@ -299,17 +299,16 @@ def tile_deepgmm_pa_kernel(
                 )
 
         def fold(src, k, opens, closes):
-            for b in range(ROW_TILES // 4):
-                for jj in range(4):
-                    for c in range(D_CHUNKS):
-                        nc.tensor.matmul(
-                            out=banks[k][b][:, jj, :],
-                            lhsT=src[:, c, part(4 * b + jj, P)],
-                            rhs=ident_f32[:],
-                            is_transpose=True,
-                            start=(opens and jj == 0 and c == 0),
-                            stop=(closes and jj == 3 and c == D_CHUNKS - 1),
-                        )
+            for c in range(D_CHUNKS):
+                for j in range(ROW_TILES):
+                    nc.tensor.matmul(
+                        out=banks[k][j // 4][:, j % 4, :],
+                        lhsT=src[:, c, part(j, P)],
+                        rhs=ident_f32[:],
+                        is_transpose=True,
+                        start=(opens and c == 0 and j % 4 == 0),
+                        stop=(closes and c == D_CHUNKS - 1 and j % 4 == 3),
+                    )
 
         def fold_logs(k):
             bank_a = psum.tile([P, 4, P], F32, tag="bank")
@@ -325,11 +324,17 @@ def tile_deepgmm_pa_kernel(
 
         for k in range(BATCH):
             logs(k)
+        nc.vector.tensor_scalar(out=mu_half[:], in0=mu_t[:], scalar1=0.5, scalar2=None, op0=ALU.mult)
+        store_rows(mu_t, out_0)
+        store_rows(sig_t, out_1)
+        for k in range(LOGS_AHEAD):
+            fold_logs(k)
         for first in range(0, CLUSTERS, BATCH):
             for k in range(first, first + BATCH):
                 inverse_squares(k)
             for k in range(first, first + BATCH):
-                fold_logs(k)
+                if k + LOGS_AHEAD < CLUSTERS:
+                    fold_logs(k + LOGS_AHEAD)
                 if scalar_squares(k):
                     weigh_squares(k)
                 else:

@@ -25,8 +25,11 @@ HALF = 512
 HALVES = ROWS // HALF
 BATCH = 4
 LOGS_AHEAD = 2
-TAIL_SQUARES = 2
+SCALAR_SQUARES = 2
+GPSIMD_SQUARES = 1
+FIRST_SQUARED = CLUSTERS - SCALAR_SQUARES - GPSIMD_SQUARES
 EPS = 0.001
+CAP = 40.0
 
 ROW_MU = 0
 ROW_SIG = CLUSTERS
@@ -47,7 +50,7 @@ def tile_deepgmm_pa_kernel(
     with ExitStack() as ctx:
         ctx.enter_context(tc.manual_schedule())
         keep = ctx.enter_context(tc.tile_pool(name="keep", bufs=1))
-        stage = ctx.enter_context(tc.tile_pool(name="stage", bufs=4))
+        stage = ctx.enter_context(tc.tile_pool(name="stage", bufs=8))
         psum = ctx.enter_context(tc.psum_pool(name="psum", bufs=8))
 
         ident_f32 = keep.tile([P, P], F32)
@@ -69,15 +72,14 @@ def tile_deepgmm_pa_kernel(
         cols = keep.tile([P, D_CHUNKS, P], F32)
         sig_t = keep.tile([P, D_CHUNKS, ROWS], F32)
         mu_t = keep.tile([P, D_CHUNKS, ROWS], F32)
-        mu_half = keep.tile([P, D_CHUNKS, ROWS], F32)
-        half_cols = keep.tile([P, D_CHUNKS, CLUSTERS], F32)
+        be_sig_less_cap = keep.tile([P, D_CHUNKS], F32)
         neg_half_cols = keep.tile([P, D_CHUNKS, CLUSTERS], F32)
         sums = keep.tile([P, CLUSTERS, ROW_TILES], F32)
 
         with ExitStack() as head:
-            codes_pool = head.enter_context(tc.tile_pool(name="codes", bufs=1))
-            soft = head.enter_context(tc.tile_pool(name="soft", bufs=1))
             load = head.enter_context(tc.tile_pool(name="load", bufs=1))
+            soft = head.enter_context(tc.tile_pool(name="soft", bufs=1))
+            codes_pool = head.enter_context(tc.tile_pool(name="codes", bufs=1))
             y_codes = codes_pool.tile([P, PASSES, ROWS], U32, align_bytes=64)
             y_scales = codes_pool.tile([P, PASSES, ROWS], U8, align_bytes=64)
             sig_codes = codes_pool.tile([P, PASSES, D], U32, align_bytes=64)
@@ -85,9 +87,12 @@ def tile_deepgmm_pa_kernel(
             mu_codes = codes_pool.tile([P, PASSES, D], U32, align_bytes=64)
             mu_scales = codes_pool.tile([P, PASSES, D], U8, align_bytes=64)
 
-            sig_raw = load.tile([P, 2 * PASSES, 2, D], BF16)
-            mu_raw = load.tile([P, 2 * PASSES, 2, D], BF16)
             y_raw = load.tile([P, ROW_TILES, KDIM], BF16)
+            y_grouped = load.tile([P, PASSES, ROWS, PACK], BF16, align_bytes=64)
+            sig_raw = load.tile([P, 2 * PASSES, 2, D], BF16)
+            sig_grouped = load.tile([P, PASSES, D, PACK], BF16, align_bytes=64)
+            mu_raw = load.tile([P, 2 * PASSES, 2, D], BF16)
+            mu_grouped = load.tile([P, PASSES, D, PACK], BF16, align_bytes=64)
             nc.sync.dma_start(
                 out=sig_raw[:], in_=We_sig.rearrange("(a q e) d -> q a e d", a=2 * PASSES, q=P, e=2)
             )
@@ -105,11 +110,11 @@ def tile_deepgmm_pa_kernel(
                 )
             nc.vector.tensor_copy(out=cols[:], in_=params_t[:])
             nc.vector.tensor_scalar(
-                out=half_cols[:],
-                in0=cols[:, :, ROW_MU : ROW_MU + CLUSTERS],
-                scalar1=0.5,
+                out=be_sig_less_cap[:],
+                in0=cols[:, :, ROW_BE_SIG],
+                scalar1=CAP,
                 scalar2=None,
-                op0=ALU.mult,
+                op0=ALU.subtract,
             )
             nc.vector.tensor_scalar(
                 out=neg_half_cols[:],
@@ -132,11 +137,9 @@ def tile_deepgmm_pa_kernel(
                         in_=grouped[:, g].rearrange("p d t -> p (d t)"),
                     )
 
-            sig_grouped = load.tile([P, PASSES, D, PACK], BF16, align_bytes=64)
             quantise_weight(sig_raw, sig_grouped, sig_codes, sig_scales)
 
             y_words = y_raw[:].bitcast(F32)
-            y_grouped = load.tile([P, PASSES, ROWS, PACK], BF16, align_bytes=64)
             y_pairs = y_grouped[:].bitcast(F32)
             for h in range(HALVES):
                 for pair in range(2 * h, 2 * h + 2):
@@ -174,35 +177,44 @@ def tile_deepgmm_pa_kernel(
                     )
                 return acc
 
-            pre = soft.tile([P, D_CHUNKS, ROWS], F32)
-            ramp = soft.tile([P, D_CHUNKS, ROWS], F32)
-            tail = soft.tile([P, D_CHUNKS, ROWS], F32)
+            curve = soft.tile([P, D_CHUNKS, ROWS], F32)
+            excess = soft.tile([P, D_CHUNKS, ROWS], F32)
+            sig_accs = {}
             for h in range(HALVES):
                 for c in range(D_CHUNKS):
-                    acc = project(sig_codes, sig_scales, c, h)
+                    sig_accs[c, h] = project(sig_codes, sig_scales, c, h)
                     nc.vector.tensor_scalar(
-                        out=pre[:, c, part(h, HALF)],
-                        in0=acc[:],
+                        out=curve[:, c, part(h, HALF)],
+                        in0=sig_accs[c, h][:],
                         scalar1=cols[:, c, ROW_BE_SIG : ROW_BE_SIG + 1],
-                        scalar2=None,
+                        scalar2=CAP,
                         op0=ALU.add,
+                        op1=ALU.min,
                     )
                     nc.scalar.activation(
-                        out=tail[:, c, part(h, HALF)], in_=pre[:, c, part(h, HALF)], func=ACT.Abs
+                        out=curve[:, c, part(h, HALF)], in_=curve[:, c, part(h, HALF)], func=ACT.Exp
                     )
-                nc.scalar.activation(
-                    out=tail[:, :, part(h, HALF)], in_=tail[:, :, part(h, HALF)], func=ACT.Exp, scale=-1.0
-                )
-            nc.vector.tensor_scalar(
-                out=ramp[:], in0=pre[:], scalar1=0.0, scalar2=EPS, op0=ALU.max, op1=ALU.add
-            )
-            mu_grouped = load.tile([P, PASSES, D, PACK], BF16, align_bytes=64)
-            quantise_weight(mu_raw, mu_grouped, mu_codes, mu_scales)
+            for h in range(HALVES):
+                for c in range(D_CHUNKS):
+                    nc.vector.tensor_scalar(
+                        out=excess[:, c, part(h, HALF)],
+                        in0=sig_accs[c, h][:],
+                        scalar1=be_sig_less_cap[:, c : c + 1],
+                        scalar2=0.0,
+                        op0=ALU.add,
+                        op1=ALU.max,
+                    )
             for c in range(D_CHUNKS):
-                nc.scalar.activation(out=tail[:, c, :], in_=tail[:, c, :], func=ACT.Ln, bias=ones_col[:])
-                nc.vector.tensor_tensor(
-                    out=sig_t[:, c, :], in0=tail[:, c, :], in1=ramp[:, c, :], op=ALU.add
+                nc.scalar.activation(out=curve[:, c, :], in_=curve[:, c, :], func=ACT.Ln, bias=ones_col[:])
+                nc.vector.scalar_tensor_tensor(
+                    out=sig_t[:, c, :],
+                    in0=curve[:, c, :],
+                    scalar=EPS,
+                    in1=excess[:, c, :],
+                    op0=ALU.add,
+                    op1=ALU.add,
                 )
+            quantise_weight(mu_raw, mu_grouped, mu_codes, mu_scales)
             for h in range(HALVES):
                 for c in range(D_CHUNKS):
                     acc = project(mu_codes, mu_scales, c, h)
@@ -225,12 +237,16 @@ def tile_deepgmm_pa_kernel(
                 nc.vector.tensor_copy(out=rows_sb[:], in_=rows_t[:])
                 nc.sync.dma_start(out=dst[part(j, P), :], in_=rows_sb[:])
 
-        log_ring = ctx.enter_context(tc.tile_pool(name="log_ring", bufs=6))
-        term_ring = ctx.enter_context(tc.tile_pool(name="term_ring", bufs=4))
+        log_ring = ctx.enter_context(tc.tile_pool(name="log_ring", bufs=5, reuse_waits="tile"))
+        term_ring = ctx.enter_context(tc.tile_pool(name="term_ring", bufs=4, reuse_waits="tile"))
+        square_pool = ctx.enter_context(tc.tile_pool(name="square_pool", bufs=GPSIMD_SQUARES, reuse_waits="tile"))
         log_tiles = {}
         term_tiles = {}
         square_tiles = {}
         banks = {}
+
+        def scalar_squares(k):
+            return CLUSTERS - SCALAR_SQUARES <= k < CLUSTERS
 
         def logs(k):
             log_std = log_ring.tile([P, D_CHUNKS, ROWS], F32)
@@ -246,13 +262,11 @@ def tile_deepgmm_pa_kernel(
         def inverse_squares(k):
             term = term_ring.tile([P, D_CHUNKS, ROWS], F32)
             term_tiles[k] = term
+            power = -2.0 if k >= FIRST_SQUARED else -1.0
             for c in range(D_CHUNKS):
                 nc.scalar.activation(
-                    out=term[:, c, :], in_=log_tiles[k][:, c, :], func=ACT.Exp, scale=-2.0
+                    out=term[:, c, :], in_=log_tiles[k][:, c, :], func=ACT.Exp, scale=power
                 )
-
-        def scalar_squares(k):
-            return CLUSTERS - TAIL_SQUARES <= k < CLUSTERS
 
         def quarter_squares(k):
             quarter = log_ring.tile([P, D_CHUNKS, ROWS], F32, tag="log_std")
@@ -260,9 +274,27 @@ def tile_deepgmm_pa_kernel(
             for c in range(D_CHUNKS):
                 nc.scalar.activation(
                     out=quarter[:, c, :],
-                    in_=mu_half[:, c, :],
+                    in_=mu_t[:, c, :],
                     func=ACT.Square,
+                    scale=0.5,
                     bias=neg_half_cols[:, c, k : k + 1],
+                )
+
+        def gpsimd_squares(k):
+            quarter = square_pool.tile([P, D_CHUNKS, ROWS], F32)
+            square_tiles[k] = quarter
+            for c in range(D_CHUNKS):
+                nc.gpsimd.tensor_scalar(
+                    out=quarter[:, c, :],
+                    in0=mu_t[:, c, :],
+                    scalar1=0.5,
+                    scalar2=neg_half_cols[:, c, k : k + 1],
+                    op0=ALU.mult,
+                    op1=ALU.add,
+                )
+            for c in range(D_CHUNKS):
+                nc.gpsimd.tensor_tensor(
+                    out=quarter[:, c, :], in0=quarter[:, c, :], in1=quarter[:, c, :], op=ALU.mult
                 )
 
         def weigh_squares(k):
@@ -291,10 +323,10 @@ def tile_deepgmm_pa_kernel(
             for c in range(D_CHUNKS):
                 nc.vector.scalar_tensor_tensor(
                     out=term[:, c, :],
-                    in0=mu_half[:, c, :],
-                    scalar=half_cols[:, c, k : k + 1],
+                    in0=term[:, c, :],
+                    scalar=0.5,
                     in1=term[:, c, :],
-                    op0=ALU.subtract,
+                    op0=ALU.mult,
                     op1=ALU.mult,
                 )
 
@@ -324,7 +356,8 @@ def tile_deepgmm_pa_kernel(
 
         for k in range(BATCH):
             logs(k)
-        nc.vector.tensor_scalar(out=mu_half[:], in0=mu_t[:], scalar1=0.5, scalar2=None, op0=ALU.mult)
+        for k in range(FIRST_SQUARED, FIRST_SQUARED + GPSIMD_SQUARES):
+            gpsimd_squares(k)
         store_rows(mu_t, out_0)
         store_rows(sig_t, out_1)
         for k in range(LOGS_AHEAD):
@@ -335,7 +368,7 @@ def tile_deepgmm_pa_kernel(
             for k in range(first, first + BATCH):
                 if k + LOGS_AHEAD < CLUSTERS:
                     fold_logs(k + LOGS_AHEAD)
-                if scalar_squares(k):
+                if k >= FIRST_SQUARED:
                     weigh_squares(k)
                 else:
                     weigh(k)

@@ -23,11 +23,18 @@ PACK = 4
 PASSES = KDIM // (P * PACK)
 HALF = 512
 HALVES = ROWS // HALF
+PSUM_BANKS = 8
+TILES_PER_BANK = HALF // P
+BANKS_PER_CLUSTER = ROW_TILES // TILES_PER_BANK
+PAIRS_PER_HALF = HALF // (2 * P)
+
 BATCH = 4
-LOGS_AHEAD = 2
+LOGS_AHEAD = PSUM_BANKS // BANKS_PER_CLUSTER - 2
 SCALAR_SQUARES = 2
 GPSIMD_SQUARES = 1
 FIRST_SQUARED = CLUSTERS - SCALAR_SQUARES - GPSIMD_SQUARES
+LOG_TILES = BATCH + 1
+
 EPS = 0.001
 CAP = 40.0
 
@@ -50,8 +57,8 @@ def tile_deepgmm_pa_kernel(
     with ExitStack() as ctx:
         ctx.enter_context(tc.manual_schedule())
         keep = ctx.enter_context(tc.tile_pool(name="keep", bufs=1))
-        stage = ctx.enter_context(tc.tile_pool(name="stage", bufs=8))
-        psum = ctx.enter_context(tc.psum_pool(name="psum", bufs=8))
+        stage = ctx.enter_context(tc.tile_pool(name="stage", bufs=ROW_TILES))
+        psum = ctx.enter_context(tc.psum_pool(name="psum", bufs=PSUM_BANKS))
 
         ident_f32 = keep.tile([P, P], F32)
         make_identity(nc, ident_f32[:])
@@ -142,7 +149,7 @@ def tile_deepgmm_pa_kernel(
             y_words = y_raw[:].bitcast(F32)
             y_pairs = y_grouped[:].bitcast(F32)
             for h in range(HALVES):
-                for pair in range(2 * h, 2 * h + 2):
+                for pair in range(PAIRS_PER_HALF * h, PAIRS_PER_HALF * (h + 1)):
                     for g in range(PASSES):
                         y_t = psum.tile([P, 2, 2 * P], F32, tag="bank")
                         for u in range(2):
@@ -215,8 +222,8 @@ def tile_deepgmm_pa_kernel(
                     op1=ALU.add,
                 )
             quantise_weight(mu_raw, mu_grouped, mu_codes, mu_scales)
-            for h in range(HALVES):
-                for c in range(D_CHUNKS):
+            for c in range(D_CHUNKS):
+                for h in range(HALVES):
                     acc = project(mu_codes, mu_scales, c, h)
                     nc.vector.tensor_scalar(
                         out=mu_t[:, c, part(h, HALF)],
@@ -237,8 +244,8 @@ def tile_deepgmm_pa_kernel(
                 nc.vector.tensor_copy(out=rows_sb[:], in_=rows_t[:])
                 nc.sync.dma_start(out=dst[part(j, P), :], in_=rows_sb[:])
 
-        log_ring = ctx.enter_context(tc.tile_pool(name="log_ring", bufs=5, reuse_waits="tile"))
-        term_ring = ctx.enter_context(tc.tile_pool(name="term_ring", bufs=4, reuse_waits="tile"))
+        log_ring = ctx.enter_context(tc.tile_pool(name="log_ring", bufs=LOG_TILES, reuse_waits="tile"))
+        term_ring = ctx.enter_context(tc.tile_pool(name="term_ring", bufs=BATCH, reuse_waits="tile"))
         square_pool = ctx.enter_context(tc.tile_pool(name="square_pool", bufs=GPSIMD_SQUARES, reuse_waits="tile"))
         log_tiles = {}
         term_tiles = {}
@@ -259,7 +266,7 @@ def tile_deepgmm_pa_kernel(
                     bias=cols[:, c, ROW_SIG + k : ROW_SIG + k + 1],
                 )
 
-        def inverse_squares(k):
+        def inverse_powers(k):
             term = term_ring.tile([P, D_CHUNKS, ROWS], F32)
             term_tiles[k] = term
             power = -2.0 if k >= FIRST_SQUARED else -1.0
@@ -268,7 +275,7 @@ def tile_deepgmm_pa_kernel(
                     out=term[:, c, :], in_=log_tiles[k][:, c, :], func=ACT.Exp, scale=power
                 )
 
-        def quarter_squares(k):
+        def quarter_squares_on_scalar(k):
             quarter = log_ring.tile([P, D_CHUNKS, ROWS], F32, tag="log_std")
             square_tiles[k] = quarter
             for c in range(D_CHUNKS):
@@ -280,7 +287,7 @@ def tile_deepgmm_pa_kernel(
                     bias=neg_half_cols[:, c, k : k + 1],
                 )
 
-        def gpsimd_squares(k):
+        def quarter_squares_on_gpsimd(k):
             quarter = square_pool.tile([P, D_CHUNKS, ROWS], F32)
             square_tiles[k] = quarter
             for c in range(D_CHUNKS):
@@ -334,37 +341,37 @@ def tile_deepgmm_pa_kernel(
             for c in range(D_CHUNKS):
                 for j in range(ROW_TILES):
                     nc.tensor.matmul(
-                        out=banks[k][j // 4][:, j % 4, :],
+                        out=banks[k][j // TILES_PER_BANK][:, j % TILES_PER_BANK, :],
                         lhsT=src[:, c, part(j, P)],
                         rhs=ident_f32[:],
                         is_transpose=True,
-                        start=(opens and c == 0 and j % 4 == 0),
-                        stop=(closes and c == D_CHUNKS - 1 and j % 4 == 3),
+                        start=(opens and c == 0 and j % TILES_PER_BANK == 0),
+                        stop=(closes and c == D_CHUNKS - 1 and j % TILES_PER_BANK == TILES_PER_BANK - 1),
                     )
 
         def fold_logs(k):
-            bank_a = psum.tile([P, 4, P], F32, tag="bank")
-            bank_b = psum.tile([P, 4, P], F32, tag="bank")
+            bank_a = psum.tile([P, TILES_PER_BANK, P], F32, tag="bank")
+            bank_b = psum.tile([P, TILES_PER_BANK, P], F32, tag="bank")
             banks[k] = [bank_a, bank_b]
             fold(log_tiles[k], k, True, False)
 
         def finish_sums(k):
-            for b in range(ROW_TILES // 4):
+            for b in range(BANKS_PER_CLUSTER):
                 nc.vector.tensor_reduce(
-                    out=sums[:, k, part(b, 4)], in_=banks[k][b][:], axis=AX.X, op=ALU.add
+                    out=sums[:, k, part(b, TILES_PER_BANK)], in_=banks[k][b][:], axis=AX.X, op=ALU.add
                 )
 
         for k in range(BATCH):
             logs(k)
         for k in range(FIRST_SQUARED, FIRST_SQUARED + GPSIMD_SQUARES):
-            gpsimd_squares(k)
+            quarter_squares_on_gpsimd(k)
         store_rows(mu_t, out_0)
         store_rows(sig_t, out_1)
         for k in range(LOGS_AHEAD):
             fold_logs(k)
         for first in range(0, CLUSTERS, BATCH):
             for k in range(first, first + BATCH):
-                inverse_squares(k)
+                inverse_powers(k)
             for k in range(first, first + BATCH):
                 if k + LOGS_AHEAD < CLUSTERS:
                     fold_logs(k + LOGS_AHEAD)
@@ -376,7 +383,7 @@ def tile_deepgmm_pa_kernel(
                 if k + BATCH < CLUSTERS:
                     logs(k + BATCH)
                 elif scalar_squares(k + 1):
-                    quarter_squares(k + 1)
+                    quarter_squares_on_scalar(k + 1)
                 if k >= 1:
                     finish_sums(k - 1)
         finish_sums(CLUSTERS - 1)

@@ -131,12 +131,7 @@ def tile_deepgmm_pa_kernel(
                 op0=ALU.mult,
             )
 
-            def quantise_weight(raw, grouped, codes, scales):
-                for g in range(PASSES):
-                    nc.vector.tensor_copy(
-                        out=grouped[:, g].rearrange("p d (u e) -> p d u e", u=2),
-                        in_=raw[:, part(g, 2)].rearrange("p u e d -> p d u e"),
-                    )
+            def quantise_weight(grouped, codes, scales):
                 for g in range(PASSES):
                     nc.vector.quantize_mx(
                         out=codes[:, g, :].bitcast(FP8X4),
@@ -144,7 +139,21 @@ def tile_deepgmm_pa_kernel(
                         in_=grouped[:, g].rearrange("p d t -> p (d t)"),
                     )
 
-            quantise_weight(sig_raw, sig_grouped, sig_codes, sig_scales)
+            for g in range(PASSES):
+                nc.vector.tensor_copy(
+                    out=sig_grouped[:, g].rearrange("p d (u e) -> p d u e", u=2),
+                    in_=sig_raw[:, part(g, 2)].rearrange("p u e d -> p d u e"),
+                )
+            quantise_weight(sig_grouped, sig_codes, sig_scales)
+            for g in range(PASSES):
+                nc.gpsimd.tensor_scalar(
+                    out=mu_grouped[:, g].rearrange("p d (u e) -> p d u e", u=2),
+                    in0=mu_raw[:, part(g, 2)].rearrange("p u e d -> p d u e"),
+                    scalar1=1.0,
+                    scalar2=0.0,
+                    op0=ALU.mult,
+                    op1=ALU.add,
+                )
 
             y_words = y_raw[:].bitcast(F32)
             y_pairs = y_grouped[:].bitcast(F32)
@@ -221,7 +230,7 @@ def tile_deepgmm_pa_kernel(
                     op0=ALU.add,
                     op1=ALU.add,
                 )
-            quantise_weight(mu_raw, mu_grouped, mu_codes, mu_scales)
+            quantise_weight(mu_grouped, mu_codes, mu_scales)
             for c in range(D_CHUNKS):
                 for h in range(HALVES):
                     acc = project(mu_codes, mu_scales, c, h)

from contextlib import ExitStack

import concourse.mybir as mybir
from concourse.masks import make_identity

F32 = mybir.dt.float32
BF16 = mybir.dt.bfloat16
U32 = mybir.dt.uint32
U8 = mybir.dt.uint8
FP8X4 = mybir.dt.float8_e4m3fn_x4
ACT = mybir.ActivationFunctionType
ALU = mybir.AluOpType
AX = mybir.AxisListType

P = 128
ROWS = 1024
KDIM = 1024
D = 512
CLUSTERS = 16
ROW_TILES = ROWS // P
D_CHUNKS = D // P
PACK = 4
PASSES = KDIM // (P * PACK)
HALF = 512
HALVES = ROWS // HALF
PSUM_BANKS = 8
TILES_PER_BANK = HALF // P
BANKS_PER_CLUSTER = ROW_TILES // TILES_PER_BANK
PAIRS_PER_HALF = HALF // (2 * P)

BATCH = 4
LOGS_AHEAD = PSUM_BANKS // BANKS_PER_CLUSTER - 2
SCALAR_SQUARES = 2
GPSIMD_SQUARES = 1
FIRST_SQUARED = CLUSTERS - SCALAR_SQUARES - GPSIMD_SQUARES
LOG_TILES = BATCH + 1

EPS = 0.001
CAP = 40.0

ROW_MU = 0
ROW_SIG = CLUSTERS
ROW_BE_MU = 2 * CLUSTERS
ROW_BE_SIG = 2 * CLUSTERS + 1

FLOPS = 2 * 2 * ROWS * KDIM * D


def part(i, size):
    return slice(i * size, (i + 1) * size)


def tile_deepgmm_pa_kernel(
    tc, Y, We_mu, be_mu, We_sig, be_sig, phi_mus, phi_sigs, phi_logits, out_0, out_1, out_2
):
    nc = tc.nc
    with ExitStack() as ctx:
        ctx.enter_context(tc.manual_schedule())
        keep = ctx.enter_context(tc.tile_pool(name="keep", bufs=1))
        stage = ctx.enter_context(tc.tile_pool(name="stage", bufs=ROW_TILES))
        psum = ctx.enter_context(tc.psum_pool(name="psum", bufs=PSUM_BANKS))

        ident_f32 = keep.tile([P, P], F32)
        make_identity(nc, ident_f32[:])
        ident_bf16 = keep.tile([P, P], BF16)
        make_identity(nc, ident_bf16[:])
        ones_col = keep.tile([P, 1], F32)
        nc.vector.memset(ones_col[:], 1.0)

        param_rows = keep.tile([P, D], BF16)
        nc.vector.memset(param_rows[:], 0.0)
        nc.scalar.dma_start(out=param_rows[ROW_MU : ROW_MU + CLUSTERS, :], in_=phi_mus)
        nc.scalar.dma_start(out=param_rows[ROW_SIG : ROW_SIG + CLUSTERS, :], in_=phi_sigs)
        nc.scalar.dma_start(out=param_rows[ROW_BE_MU : ROW_BE_MU + 1, :], in_=be_mu.unsqueeze(0))
        nc.scalar.dma_start(out=param_rows[ROW_BE_SIG : ROW_BE_SIG + 1, :], in_=be_sig.unsqueeze(0))
        logits_bc = keep.tile([P, CLUSTERS], BF16)
        nc.scalar.dma_start(out=logits_bc[:], in_=phi_logits.partition_broadcast(P))

        cols = keep.tile([P, D_CHUNKS, P], F32)
        sig_t = keep.tile([P, D_CHUNKS, ROWS], F32)
        mu_t = keep.tile([P, D_CHUNKS, ROWS], F32)
        be_sig_less_cap = keep.tile([P, D_CHUNKS], F32)
        neg_half_cols = keep.tile([P, D_CHUNKS, CLUSTERS], F32)
        sums = keep.tile([P, CLUSTERS, ROW_TILES], F32)

        with ExitStack() as head:
            load = head.enter_context(tc.tile_pool(name="load", bufs=1))
            soft = head.enter_context(tc.tile_pool(name="soft", bufs=1))
            codes_pool = head.enter_context(tc.tile_pool(name="codes", bufs=1))
            y_codes = codes_pool.tile([P, PASSES, ROWS], U32, align_bytes=64)
            y_scales = codes_pool.tile([P, PASSES, ROWS], U8, align_bytes=64)
            sig_codes = codes_pool.tile([P, PASSES, D], U32, align_bytes=64)
            sig_scales = codes_pool.tile([P, PASSES, D], U8, align_bytes=64)
            mu_codes = codes_pool.tile([P, PASSES, D], U32, align_bytes=64)
            mu_scales = codes_pool.tile([P, PASSES, D], U8, align_bytes=64)

            y_raw = load.tile([P, ROW_TILES, KDIM], BF16)
            y_grouped = load.tile([P, PASSES, ROWS, PACK], BF16, align_bytes=64)
            sig_raw = load.tile([P, 2 * PASSES, 2, D], BF16)
            sig_grouped = load.tile([P, PASSES, D, PACK], BF16, align_bytes=64)
            mu_raw = load.tile([P, 2 * PASSES, 2, D], BF16)
            mu_grouped = load.tile([P, PASSES, D, PACK], BF16, align_bytes=64)
            nc.sync.dma_start(
                out=sig_raw[:], in_=We_sig.rearrange("(a q e) d -> q a e d", a=2 * PASSES, q=P, e=2)
            )
            y_view = Y.rearrange("(j p) y -> p j y", p=P)
            for pair in range(ROW_TILES // 2):
                nc.sync.dma_start(out=y_raw[:, part(pair, 2), :], in_=y_view[:, part(pair, 2), :])
            nc.sync.dma_start(
                out=mu_raw[:], in_=We_mu.rearrange("(a q e) d -> q a e d", a=2 * PASSES, q=P, e=2)
            )

            params_t = psum.tile([P, D_CHUNKS, P], BF16, tag="bank")
            for c in range(D_CHUNKS):
                nc.tensor.transpose(
                    out=params_t[:, c, :], in_=param_rows[:, part(c, P)], identity=ident_bf16[:]
                )
            nc.vector.tensor_copy(out=cols[:], in_=params_t[:])
            nc.vector.tensor_scalar(
                out=be_sig_less_cap[:],
                in0=cols[:, :, ROW_BE_SIG],
                scalar1=CAP,
                scalar2=None,
                op0=ALU.subtract,
            )
            nc.vector.tensor_scalar(
                out=neg_half_cols[:],
                in0=cols[:, :, ROW_MU : ROW_MU + CLUSTERS],
                scalar1=-0.5,
                scalar2=None,
                op0=ALU.mult,
            )

            def quantise_weight(grouped, codes, scales):
                for g in range(PASSES):
                    nc.vector.quantize_mx(
                        out=codes[:, g, :].bitcast(FP8X4),
                        scales=scales[:, g, :],
                        in_=grouped[:, g].rearrange("p d t -> p (d t)"),
                    )

            for g in range(PASSES):
                nc.vector.tensor_copy(
                    out=sig_grouped[:, g].rearrange("p d (u e) -> p d u e", u=2),
                    in_=sig_raw[:, part(g, 2)].rearrange("p u e d -> p d u e"),
                )
            quantise_weight(sig_grouped, sig_codes, sig_scales)
            for g in range(PASSES):
                nc.gpsimd.tensor_scalar(
                    out=mu_grouped[:, g].rearrange("p d (u e) -> p d u e", u=2),
                    in0=mu_raw[:, part(g, 2)].rearrange("p u e d -> p d u e"),
                    scalar1=1.0,
                    scalar2=0.0,
                    op0=ALU.mult,
                    op1=ALU.add,
                )

            y_words = y_raw[:].bitcast(F32)
            y_pairs = y_grouped[:].bitcast(F32)
            for h in range(HALVES):
                for pair in range(PAIRS_PER_HALF * h, PAIRS_PER_HALF * (h + 1)):
                    for g in range(PASSES):
                        y_t = psum.tile([P, 2, 2 * P], F32, tag="bank")
                        for u in range(2):
                            for jj in range(2):
                                nc.tensor.transpose(
                                    out=y_t[:, u, part(jj, P)],
                                    in_=y_words[:, 2 * pair + jj, part(2 * g + u, P)],
                                    identity=ident_f32[:],
                                )
                        nc.scalar.copy(
                            out=y_pairs[:, g, part(pair, 2 * P), :],
                            in_=y_t[:].rearrange("p u n -> p n u"),
                        )
                for g in range(PASSES):
                    nc.vector.quantize_mx(
                        out=y_codes[:, g, part(h, HALF)].bitcast(FP8X4),
                        scales=y_scales[:, g, part(h, HALF)],
                        in_=y_grouped[:, g, part(h, HALF), :].rearrange("p n t -> p (n t)"),
                    )

            def project(codes, scales, c, h):
                acc = psum.tile([P, HALF], F32, tag="bank")
                for g in range(PASSES):
                    nc.tensor.matmul_mx(
                        out=acc[:],
                        lhsT=codes[:, g, part(c, P)].bitcast(FP8X4),
                        lhsT_scale=scales[:, g, part(c, P)],
                        rhs=y_codes[:, g, part(h, HALF)].bitcast(FP8X4),
                        rhs_scale=y_scales[:, g, part(h, HALF)],
                        start=(g == 0),
                        stop=(g == PASSES - 1),
                    )
                return acc

            curve = soft.tile([P, D_CHUNKS, ROWS], F32)
            excess = soft.tile([P, D_CHUNKS, ROWS], F32)
            sig_accs = {}
            for h in range(HALVES):
                for c in range(D_CHUNKS):
                    sig_accs[c, h] = project(sig_codes, sig_scales, c, h)
                    nc.vector.tensor_scalar(
                        out=curve[:, c, part(h, HALF)],
                        in0=sig_accs[c, h][:],
                        scalar1=cols[:, c, ROW_BE_SIG : ROW_BE_SIG + 1],
                        scalar2=CAP,
                        op0=ALU.add,
                        op1=ALU.min,
                    )
                    nc.scalar.activation(
                        out=curve[:, c, part(h, HALF)], in_=curve[:, c, part(h, HALF)], func=ACT.Exp
                    )
            for h in range(HALVES):
                for c in range(D_CHUNKS):
                    nc.vector.tensor_scalar(
                        out=excess[:, c, part(h, HALF)],
                        in0=sig_accs[c, h][:],
                        scalar1=be_sig_less_cap[:, c : c + 1],
                        scalar2=0.0,
                        op0=ALU.add,
                        op1=ALU.max,
                    )
            for c in range(D_CHUNKS):
                nc.scalar.activation(out=curve[:, c, :], in_=curve[:, c, :], func=ACT.Ln, bias=ones_col[:])
                nc.vector.scalar_tensor_tensor(
                    out=sig_t[:, c, :],
                    in0=curve[:, c, :],
                    scalar=EPS,
                    in1=excess[:, c, :],
                    op0=ALU.add,
                    op1=ALU.add,
                )
            quantise_weight(mu_grouped, mu_codes, mu_scales)
            for c in range(D_CHUNKS):
                for h in range(HALVES):
                    acc = project(mu_codes, mu_scales, c, h)
                    nc.vector.tensor_scalar(
                        out=mu_t[:, c, part(h, HALF)],
                        in0=acc[:],
                        scalar1=cols[:, c, ROW_BE_MU : ROW_BE_MU + 1],
                        scalar2=None,
                        op0=ALU.add,
                    )

        def store_rows(src, dst):
            for j in range(ROW_TILES):
                rows_t = psum.tile([P, D], F32, tag="bank")
                for c in range(D_CHUNKS):
                    nc.tensor.transpose(
                        out=rows_t[:, part(c, P)], in_=src[:, c, part(j, P)], identity=ident_f32[:]
                    )
                rows_sb = stage.tile([P, D], F32)
                nc.vector.tensor_copy(out=rows_sb[:], in_=rows_t[:])
                nc.sync.dma_start(out=dst[part(j, P), :], in_=rows_sb[:])

        log_ring = ctx.enter_context(tc.tile_pool(name="log_ring", bufs=LOG_TILES, reuse_waits="tile"))
        term_ring = ctx.enter_context(tc.tile_pool(name="term_ring", bufs=BATCH, reuse_waits="tile"))
        square_pool = ctx.enter_context(tc.tile_pool(name="square_pool", bufs=GPSIMD_SQUARES, reuse_waits="tile"))
        log_tiles = {}
        term_tiles = {}
        square_tiles = {}
        banks = {}

        def scalar_squares(k):
            return CLUSTERS - SCALAR_SQUARES <= k < CLUSTERS

        def logs(k):
            log_std = log_ring.tile([P, D_CHUNKS, ROWS], F32)
            log_tiles[k] = log_std
            for c in range(D_CHUNKS):
                nc.scalar.activation(
                    out=log_std[:, c, :],
                    in_=sig_t[:, c, :],
                    func=ACT.Ln,
                    bias=cols[:, c, ROW_SIG + k : ROW_SIG + k + 1],
                )

        def inverse_powers(k):
            term = term_ring.tile([P, D_CHUNKS, ROWS], F32)
            term_tiles[k] = term
            power = -2.0 if k >= FIRST_SQUARED else -1.0
            for c in range(D_CHUNKS):
                nc.scalar.activation(
                    out=term[:, c, :], in_=log_tiles[k][:, c, :], func=ACT.Exp, scale=power
                )

        def quarter_squares_on_scalar(k):
            quarter = log_ring.tile([P, D_CHUNKS, ROWS], F32, tag="log_std")
            square_tiles[k] = quarter
            for c in range(D_CHUNKS):
                nc.scalar.activation(
                    out=quarter[:, c, :],
                    in_=mu_t[:, c, :],
                    func=ACT.Square,
                    scale=0.5,
                    bias=neg_half_cols[:, c, k : k + 1],
                )

        def quarter_squares_on_gpsimd(k):
            quarter = square_pool.tile([P, D_CHUNKS, ROWS], F32)
            square_tiles[k] = quarter
            for c in range(D_CHUNKS):
                nc.gpsimd.tensor_scalar(
                    out=quarter[:, c, :],
                    in0=mu_t[:, c, :],
                    scalar1=0.5,
                    scalar2=neg_half_cols[:, c, k : k + 1],
                    op0=ALU.mult,
                    op1=ALU.add,
                )
            for c in range(D_CHUNKS):
                nc.gpsimd.tensor_tensor(
                    out=quarter[:, c, :], in0=quarter[:, c, :], in1=quarter[:, c, :], op=ALU.mult
                )

        def weigh_squares(k):
            term = term_tiles[k]
            for c in range(D_CHUNKS):
                nc.vector.scalar_tensor_tensor(
                    out=term[:, c, :],
                    in0=square_tiles[k][:, c, :],
                    scalar=2.0,
                    in1=term[:, c, :],
                    op0=ALU.mult,
                    op1=ALU.mult,
                )

        def weigh(k):
            term = term_tiles[k]
            for c in range(D_CHUNKS):
                nc.vector.scalar_tensor_tensor(
                    out=term[:, c, :],
                    in0=mu_t[:, c, :],
                    scalar=cols[:, c, ROW_MU + k : ROW_MU + k + 1],
                    in1=term[:, c, :],
                    op0=ALU.subtract,
                    op1=ALU.mult,
                )
            for c in range(D_CHUNKS):
                nc.vector.scalar_tensor_tensor(
                    out=term[:, c, :],
                    in0=term[:, c, :],
                    scalar=0.5,
                    in1=term[:, c, :],
                    op0=ALU.mult,
                    op1=ALU.mult,
                )

        def fold(src, k, opens, closes):
            for c in range(D_CHUNKS):
                for j in range(ROW_TILES):
                    nc.tensor.matmul(
                        out=banks[k][j // TILES_PER_BANK][:, j % TILES_PER_BANK, :],
                        lhsT=src[:, c, part(j, P)],
                        rhs=ident_f32[:],
                        is_transpose=True,
                        start=(opens and c == 0 and j % TILES_PER_BANK == 0),
                        stop=(closes and c == D_CHUNKS - 1 and j % TILES_PER_BANK == TILES_PER_BANK - 1),
                    )

        def fold_logs(k):
            bank_a = psum.tile([P, TILES_PER_BANK, P], F32, tag="bank")
            bank_b = psum.tile([P, TILES_PER_BANK, P], F32, tag="bank")
            banks[k] = [bank_a, bank_b]
            fold(log_tiles[k], k, True, False)

        def finish_sums(k):
            for b in range(BANKS_PER_CLUSTER):
                nc.vector.tensor_reduce(
                    out=sums[:, k, part(b, TILES_PER_BANK)], in_=banks[k][b][:], axis=AX.X, op=ALU.add
                )

        for k in range(BATCH):
            logs(k)
        for k in range(FIRST_SQUARED, FIRST_SQUARED + GPSIMD_SQUARES):
            quarter_squares_on_gpsimd(k)
        store_rows(mu_t, out_0)
        store_rows(sig_t, out_1)
        for k in range(LOGS_AHEAD):
            fold_logs(k)
        for first in range(0, CLUSTERS, BATCH):
            for k in range(first, first + BATCH):
                inverse_powers(k)
            for k in range(first, first + BATCH):
                if k + LOGS_AHEAD < CLUSTERS:
                    fold_logs(k + LOGS_AHEAD)
                if k >= FIRST_SQUARED:
                    weigh_squares(k)
                else:
                    weigh(k)
                fold(term_tiles[k], k, False, True)
                if k + BATCH < CLUSTERS:
                    logs(k + BATCH)
                elif scalar_squares(k + 1):
                    quarter_squares_on_scalar(k + 1)
                if k >= 1:
                    finish_sums(k - 1)
        finish_sums(CLUSTERS - 1)

        shape = [P, ROW_TILES, CLUSTERS]
        z = keep.tile(shape, F32)
        nc.vector.tensor_tensor(
            out=z[:],
            in0=logits_bc[:].unsqueeze(1).to_broadcast(shape),
            in1=sums[:].rearrange("p k j -> p j k"),
            op=ALU.subtract,
        )
        top = keep.tile([P, ROW_TILES], F32)
        nc.vector.tensor_reduce(out=top[:], in_=z[:], axis=AX.X, op=ALU.max)
        nc.vector.tensor_tensor(
            out=z[:], in0=z[:], in1=top[:].unsqueeze(2).to_broadcast(shape), op=ALU.subtract
        )
        weights = keep.tile(shape, F32)
        nc.scalar.activation(out=weights[:], in_=z[:], func=ACT.Exp)
        norm = keep.tile([P, ROW_TILES], F32)
        nc.vector.tensor_reduce(out=norm[:], in_=weights[:], axis=AX.X, op=ALU.add)
        nc.scalar.activation(out=norm[:], in_=norm[:], func=ACT.Ln)
        nc.vector.tensor_tensor(
            out=z[:], in0=z[:], in1=norm[:].unsqueeze(2).to_broadcast(shape), op=ALU.subtract
        )
        nc.sync.dma_start(out=out_2.rearrange("(j p) k -> p j k", p=P), in_=z[:])
